import numpy as np
import ml_dtypes

BF16 = ml_dtypes.bfloat16


def bf(x):
    return np.asarray(x, np.float32).astype(BF16)


def f32(x):
    return np.asarray(x, np.float32)


def f64(x):
    return np.asarray(x).astype(np.float64)


def striped(idx):
    return np.tile(idx.reshape(-1, 16).T, (8, 1))


C, S, H, W, GH, N = 128, 1024, 32, 64, 128, 2048
OFFSETS = [(-4, -4), (-4, -1), (-4, 2), (-3, 4), (-2, -3), (2, 3), (3, -2), (4, 4)]


def sigmoid(v):
    return 1.0 / (1.0 + np.exp(-v))


def setup_inputs():
    return {
        "table": bf(np.random.standard_normal((C, S))),
        "wm": bf(2.0 * np.random.standard_normal((C, C)) / np.sqrt(C)),
        "bm": f32(0.1 * np.random.standard_normal((C, 1))),
        "wx": bf(np.random.standard_normal((C, GH)) / np.sqrt(C + C)),
        "wa": bf(np.random.standard_normal((C, GH)) / np.sqrt(C + C)),
        "bh": f32(0.1 * np.random.standard_normal((GH, 1))),
        "wz": bf(2.0 * np.random.standard_normal((GH, C)) / np.sqrt(GH)),
        "bz": f32(0.1 * np.random.standard_normal((C, 1))),
        "offs": striped(np.random.permutation(np.tile(np.arange(S), 2))[:N]),
    }


def reference(table, wm, bm, wx, wa, bh, wz, bz, offs):
    idx = offs[:16].T.reshape(-1)
    xp = f64(table)[:, idx]
    msg = (f64(wm).T @ xp + f64(bm)).reshape(C, H, W)
    agg = np.zeros((C, H, W), np.float64)
    for dy, dx in OFFSETS:
        agg = agg + np.roll(msg, (dy, dx), axis=(1, 2))
    agg = agg.reshape(C, N) / len(OFFSETS)
    hidden = np.maximum(f64(wx).T @ xp + f64(wa).T @ agg + f64(bh), 0.0)
    gate = sigmoid(f64(wz).T @ hidden + f64(bz))
    return agg * gate

@@ -1,0 +1,228 @@
+import concourse.mybir as mybir
+from concourse.masks import make_identity
+
+F32 = mybir.dt.float32
+BF16 = mybir.dt.bfloat16
+U16 = mybir.dt.uint16
+ACT = mybir.ActivationFunctionType
+ALU = mybir.AluOpType
+
+P = 128
+TABLE_COLS = 1024
+GRID_ROWS, GRID_COLS = 32, 64
+N = GRID_ROWS * GRID_COLS
+ROW_OFFSETS = GRID_COLS // 16
+PSUM_BANKS = 8
+BANK_ROWS = 512 // GRID_COLS
+N_BANKS = GRID_ROWS // BANK_ROWS
+REACH = 4
+PIECES = ((4, 8), (12, 8), (20, 8), (28, 4), (32, 4))
+MSG_PARTS = ((0, 8), (8, 4), (12, 4), (16, 8), (24, 8))
+FIRST_HALVES = ((4, 4), (8, 4))
+GROUPS = ((0,), (1,), (2,), (3, 4))
+
+STEP = (2, 1)
+DUO_SHIFTS = ((-4, -4), (2, 3))
+FAR_SHIFTS = ((-4, -1), (-4, 2))
+NEAR_SHIFTS = ((-3, 4), (3, -2))
+TRIO_SHIFTS = FAR_SHIFTS + NEAR_SHIFTS
+HELPED = (2,)
+N_SHIFTS = 2 * len(DUO_SHIFTS) + len(FAR_SHIFTS) + len(NEAR_SHIFTS)
+PAD_ROWS = GRID_ROWS + 2 * REACH
+PAD_COLS = GRID_COLS + 2 * REACH
+
+FLOPS = 4 * 2 * P * P * N
+
+
+def as_grid(flat):
+    return flat.rearrange("p (r t) -> p r t", t=GRID_COLS)
+
+
+def shifted(padded, piece, shift):
+    top, n_rows = piece
+    dy, dx = shift
+    row = top - dy
+    col = REACH - dx
+    return padded[:, row : row + n_rows, col : col + GRID_COLS]
+
+
+def tile_graphaugmentation_kernel(tc, table, wm, bm, wx, wa, bh, wz, bz, offs, out):
+    nc = tc.nc
+    with (
+        tc.tile_pool(name="held", bufs=1) as held,
+        tc.tile_pool(name="work", bufs=len(PIECES)) as work,
+        tc.psum_pool(name="psum", bufs=PSUM_BANKS) as psum,
+    ):
+        offsets = held.tile([P, N // 16], U16, name="offsets")
+        nc.sync.dma_start(offsets[:], offs)
+        table_sb = held.tile([P, TABLE_COLS], BF16, name="table_sb")
+        nc.scalar.dma_start(table_sb[:], table)
+        wm_sb = held.tile([P, P], BF16, name="wm_sb")
+        nc.sync.dma_start(wm_sb[:], wm)
+        bm_sb = held.tile([P, 1], F32, name="bm_sb")
+        nc.sync.dma_start(bm_sb[:], bm)
+        wx_sb = held.tile([P, P], BF16, name="wx_sb")
+        nc.sync.dma_start(wx_sb[:], wx)
+        wa_sb = held.tile([P, P], BF16, name="wa_sb")
+        nc.sync.dma_start(wa_sb[:], wa)
+        bh_sb = held.tile([P, 1], F32, name="bh_sb")
+        nc.sync.dma_start(bh_sb[:], bh)
+        wz_sb = held.tile([P, P], BF16, name="wz_sb")
+        nc.sync.dma_start(wz_sb[:], wz)
+        bz_sb = held.tile([P, 1], F32, name="bz_sb")
+        nc.sync.dma_start(bz_sb[:], bz)
+
+        identity = held.tile([P, P], F32, name="identity")
+        make_identity(nc, identity[:])
+
+        warm = held.tile([P, 1], F32, name="warm")
+        nc.vector.memset(warm[:], 0.0)
+        nc.scalar.activation(warm[:], warm[:], ACT.Sigmoid)
+
+        share = 1.0 / N_SHIFTS
+        bm_share = held.tile([P, 1], F32, name="bm_share")
+        nc.vector.tensor_scalar_mul(bm_share[:], bm_sb[:], share)
+
+        def picked(top, n_rows):
+            return table_sb[:].indirect(offsets[:, top * ROW_OFFSETS : (top + n_rows) * ROW_OFFSETS])
+
+        msg_ps = []
+        for top, n_rows in MSG_PARTS:
+            msg_ps.append(psum.tile([P, n_rows * GRID_COLS], F32, name="msg_ps", tag="bank"))
+            nc.tensor.matmul(msg_ps[-1][:], wm_sb[:], picked(top, n_rows), start=True, stop=True)
+
+        msg_pad = held.tile([P, PAD_ROWS, PAD_COLS], F32, name="msg_pad")
+        first, last = REACH, REACH + GRID_COLS
+
+        def land(part):
+            top, n_rows = MSG_PARTS[part]
+            product = as_grid(msg_ps[part][:])
+            target = msg_pad[:, top : top + n_rows, :]
+            for to_cols, from_cols in (
+                (slice(first, last), slice(0, GRID_COLS)),
+                (slice(0, first), slice(GRID_COLS - REACH, GRID_COLS)),
+                (slice(last, PAD_COLS), slice(0, REACH)),
+            ):
+                nc.scalar.activation(
+                    target[:, :, to_cols], product[:, :, from_cols], ACT.Identity, bias=bm_share[:], scale=share
+                )
+
+        for part in range(len(MSG_PARTS)):
+            land(part)
+        nc.scalar.copy(msg_pad[:, GRID_ROWS:PAD_ROWS, :], msg_pad[:, 0 : PAD_ROWS - GRID_ROWS, :])
+
+        hidden_ps = []
+        for top, n_rows in PIECES:
+            hidden_ps.append(psum.tile([P, n_rows * GRID_COLS], F32, name="hidden_ps", tag="bank"))
+            nc.tensor.matmul(hidden_ps[-1][:], wx_sb[:], picked(top % GRID_ROWS, n_rows), start=True, stop=False)
+
+        DUO_TOP = PIECES[0][0] - STEP[0]
+        duo_pad = held.tile([P, STEP[0] + GRID_ROWS, STEP[1] + GRID_COLS], F32, name="duo_pad")
+
+        def make_duo_block(b):
+            make_duo(PIECES[0][0] + b * BANK_ROWS, PIECES[0][0] + (b + 1) * BANK_ROWS)
+
+        def make_duo(top, end):
+            terms = [
+                msg_pad[:, top - dy : end - dy, REACH - STEP[1] - dx : REACH + GRID_COLS - dx]
+                for dy, dx in DUO_SHIFTS
+            ]
+            nc.vector.tensor_tensor(duo_pad[:, top - DUO_TOP : end - DUO_TOP, :], terms[0], terms[1], ALU.add)
+
+        def duo_at(piece, back):
+            row = piece[0] - DUO_TOP - STEP[0] * back
+            col = STEP[1] * (1 - back)
+            return duo_pad[:, row : row + piece[1], col : col + GRID_COLS]
+
+        def pair_on_vector(pair, piece, rows, shifts):
+            at = rows[0] - piece[0]
+            nc.vector.tensor_tensor(
+                as_grid(pair[:])[:, at : at + rows[1], :],
+                shifted(msg_pad, rows, shifts[0]),
+                shifted(msg_pad, rows, shifts[1]),
+                ALU.add,
+            )
+
+        def sum_on_tensor(i, shifts):
+            helped[i] = psum.tile([P, PIECES[i][1] * GRID_COLS], F32, name="helped_ps", tag="bank")
+            for k, shift in enumerate(shifts):
+                nc.tensor.matmul(
+                    as_grid(helped[i][:]),
+                    identity[:],
+                    shifted(msg_pad, PIECES[i], shift),
+                    start=(k == 0),
+                    stop=(k == len(shifts) - 1),
+                )
+
+        def first_half_of_gate(i):
+            nc.tensor.matmul(hidden_ps[i][:], wa_sb[:], agg_bf[i][:], start=False, stop=True)
+            hidden_bf[i] = work.tile([P, PIECES[i][1] * GRID_COLS], BF16, name="hidden_bf")
+            nc.scalar.activation(hidden_bf[i][:], hidden_ps[i][:], ACT.Relu, bias=bh_sb[:])
+
+        def second_half_of_gate(i):
+            cells = PIECES[i][1] * GRID_COLS
+            gate_ps = psum.tile([P, cells], F32, name="gate_ps", tag="bank")
+            nc.tensor.matmul(gate_ps[:], wz_sb[:], hidden_bf[i][:], start=True, stop=True)
+            gate[i] = work.tile([P, cells], F32, name="gate")
+            nc.scalar.activation(gate[i][:], gate_ps[:], ACT.Sigmoid, bias=bz_sb[:])
+
+        far, near, helped, duos, agg, agg_bf, hidden_bf, gate = {}, {}, {}, {}, {}, {}, {}, {}
+        far[0] = work.tile([P, PIECES[0][1] * GRID_COLS], F32, name="far")
+        near[0] = work.tile([P, PIECES[0][1] * GRID_COLS], F32, name="near")
+        for h, half in enumerate(FIRST_HALVES):
+            make_duo(half[0] - (STEP[0] if h == 0 else 0), half[0] + half[1])
+            pair_on_vector(far[0], PIECES[0], half, FAR_SHIFTS)
+            pair_on_vector(near[0], PIECES[0], half, NEAR_SHIFTS)
+        for g, group in enumerate(GROUPS):
+            if g < len(HELPED):
+                sum_on_tensor(HELPED[g], TRIO_SHIFTS if PIECES[HELPED[g]][1] == BANK_ROWS else FAR_SHIFTS)
+            if g == 1 or g == 3:
+                for i in group:
+                    near[i] = work.tile([P, PIECES[i][1] * GRID_COLS], F32, name="near")
+                    pair_on_vector(near[i], PIECES[i], PIECES[i], NEAR_SHIFTS)
+            if g == 1 or g == 3:
+                for i in group:
+                    far[i] = work.tile([P, PIECES[i][1] * GRID_COLS], F32, name="far")
+                    pair_on_vector(far[i], PIECES[i], PIECES[i], FAR_SHIFTS)
+            for i in group:
+                duos[i] = work.tile([P, PIECES[i][1] * GRID_COLS], F32, name="duos")
+                nc.vector.tensor_tensor(
+                    as_grid(duos[i][:]), duo_at(PIECES[i], 0), duo_at(PIECES[i], 1), ALU.add
+                )
+            for i in group:
+                if g == 2:
+                    near[i] = helped[i]
+                else:
+                    nc.vector.tensor_tensor(near[i][:], near[i][:], far[i][:], ALU.add)
+            if g + 1 < N_BANKS:
+                make_duo_block(g + 1)
+            for i in group:
+                cells = PIECES[i][1] * GRID_COLS
+                agg[i] = work.tile([P, cells], F32, name="agg")
+                agg_bf[i] = work.tile([P, cells], BF16, name="agg_bf")
+                if PIECES[i][1] == BANK_ROWS:
+                    nc.vector.tensor_tensor(agg[i][:], duos[i][:], near[i][:], ALU.add)
+                    nc.scalar.copy(agg_bf[i][:], agg[i][:])
+                else:
+                    nc.vector.tensor_tensor(agg_bf[i][:], duos[i][:], near[i][:], ALU.add)
+
+            if g == len(GROUPS) - 1:
+                for i in group:
+                    first_half_of_gate(i)
+            if g > 0:
+                for i in GROUPS[g - 1]:
+                    second_half_of_gate(i)
+            if g < len(GROUPS) - 1:
+                for i in group:
+                    first_half_of_gate(i)
+        for i in GROUPS[-1]:
+            second_half_of_gate(i)
+
+        for i, piece in enumerate(PIECES):
+            if piece[1] != BANK_ROWS:
+                nc.vector.tensor_tensor(agg[i][:], duos[i][:], near[i][:], ALU.add)
+        for i, (top, n_rows) in enumerate(PIECES):
+            gated = work.tile([P, n_rows * GRID_COLS], F32, name="gated")
+            nc.vector.tensor_tensor(gated[:], agg[i][:], gate[i][:], ALU.mult)
+            row = top % GRID_ROWS
+            nc.sync.dma_start(out[:, row * GRID_COLS : (row + n_rows) * GRID_COLS], gated[:])

@@ -18,6 +18,7 @@ N_BANKS = GRID_ROWS // BANK_ROWS
 REACH = 4
 PIECES = ((4, 8), (12, 8), (20, 8), (28, 4), (32, 4))
 MSG_PARTS = ((0, 8), (8, 4), (12, 4), (16, 8), (24, 8))
+VECTOR_LANDS = (1,)
 FIRST_HALVES = ((4, 4), (8, 4))
 GROUPS = ((0,), (1,), (2,), (3, 4))
 
@@ -94,7 +95,7 @@ def tile_graphaugmentation_kernel(tc, table, wm, bm, wx, wa, bh, wz, bz, offs, o
         msg_pad = held.tile([P, PAD_ROWS, PAD_COLS], F32, name="msg_pad")
         first, last = REACH, REACH + GRID_COLS
 
-        def land(part):
+        def land(part, on_vector=False):
             top, n_rows = MSG_PARTS[part]
             product = as_grid(msg_ps[part][:])
             target = msg_pad[:, top : top + n_rows, :]
@@ -103,12 +104,17 @@ def tile_graphaugmentation_kernel(tc, table, wm, bm, wx, wa, bh, wz, bz, offs, o
                 (slice(0, first), slice(GRID_COLS - REACH, GRID_COLS)),
                 (slice(last, PAD_COLS), slice(0, REACH)),
             ):
-                nc.scalar.activation(
-                    target[:, :, to_cols], product[:, :, from_cols], ACT.Identity, bias=bm_share[:], scale=share
-                )
+                if on_vector:
+                    nc.vector.tensor_scalar(
+                        target[:, :, to_cols], product[:, :, from_cols], share, bm_share[:], ALU.mult, ALU.add
+                    )
+                else:
+                    nc.scalar.activation(
+                        target[:, :, to_cols], product[:, :, from_cols], ACT.Identity, bias=bm_share[:], scale=share
+                    )
 
         for part in range(len(MSG_PARTS)):
-            land(part)
+            land(part, on_vector=part in VECTOR_LANDS)
         nc.scalar.copy(msg_pad[:, GRID_ROWS:PAD_ROWS, :], msg_pad[:, 0 : PAD_ROWS - GRID_ROWS, :])
 
         hidden_ps = []

import concourse.mybir as mybir
from concourse.masks import make_identity

F32 = mybir.dt.float32
BF16 = mybir.dt.bfloat16
U16 = mybir.dt.uint16
ACT = mybir.ActivationFunctionType
ALU = mybir.AluOpType

P = 128
TABLE_COLS = 1024
GRID_ROWS, GRID_COLS = 32, 64
N = GRID_ROWS * GRID_COLS
ROW_OFFSETS = GRID_COLS // 16
PSUM_BANKS = 8
BANK_ROWS = 512 // GRID_COLS
N_BANKS = GRID_ROWS // BANK_ROWS
REACH = 4
PIECES = ((4, 8), (12, 8), (20, 8), (28, 4), (32, 4))
MSG_PARTS = ((0, 8), (8, 4), (12, 4), (16, 8), (24, 8))
VECTOR_LANDS = (1,)
FIRST_HALVES = ((4, 4), (8, 4))
GROUPS = ((0,), (1,), (2,), (3, 4))

STEP = (2, 1)
DUO_SHIFTS = ((-4, -4), (2, 3))
FAR_SHIFTS = ((-4, -1), (-4, 2))
NEAR_SHIFTS = ((-3, 4), (3, -2))
TRIO_SHIFTS = FAR_SHIFTS + NEAR_SHIFTS
HELPED = (2,)
N_SHIFTS = 2 * len(DUO_SHIFTS) + len(FAR_SHIFTS) + len(NEAR_SHIFTS)
PAD_ROWS = GRID_ROWS + 2 * REACH
PAD_COLS = GRID_COLS + 2 * REACH

FLOPS = 4 * 2 * P * P * N


def as_grid(flat):
    return flat.rearrange("p (r t) -> p r t", t=GRID_COLS)


def shifted(padded, piece, shift):
    top, n_rows = piece
    dy, dx = shift
    row = top - dy
    col = REACH - dx
    return padded[:, row : row + n_rows, col : col + GRID_COLS]


def tile_graphaugmentation_kernel(tc, table, wm, bm, wx, wa, bh, wz, bz, offs, out):
    nc = tc.nc
    with (
        tc.tile_pool(name="held", bufs=1) as held,
        tc.tile_pool(name="work", bufs=len(PIECES)) as work,
        tc.psum_pool(name="psum", bufs=PSUM_BANKS) as psum,
    ):
        offsets = held.tile([P, N // 16], U16, name="offsets")
        nc.sync.dma_start(offsets[:], offs)
        table_sb = held.tile([P, TABLE_COLS], BF16, name="table_sb")
        nc.scalar.dma_start(table_sb[:], table)
        wm_sb = held.tile([P, P], BF16, name="wm_sb")
        nc.sync.dma_start(wm_sb[:], wm)
        bm_sb = held.tile([P, 1], F32, name="bm_sb")
        nc.sync.dma_start(bm_sb[:], bm)
        wx_sb = held.tile([P, P], BF16, name="wx_sb")
        nc.sync.dma_start(wx_sb[:], wx)
        wa_sb = held.tile([P, P], BF16, name="wa_sb")
        nc.sync.dma_start(wa_sb[:], wa)
        bh_sb = held.tile([P, 1], F32, name="bh_sb")
        nc.sync.dma_start(bh_sb[:], bh)
        wz_sb = held.tile([P, P], BF16, name="wz_sb")
        nc.sync.dma_start(wz_sb[:], wz)
        bz_sb = held.tile([P, 1], F32, name="bz_sb")
        nc.sync.dma_start(bz_sb[:], bz)

        identity = held.tile([P, P], F32, name="identity")
        make_identity(nc, identity[:])

        warm = held.tile([P, 1], F32, name="warm")
        nc.vector.memset(warm[:], 0.0)
        nc.scalar.activation(warm[:], warm[:], ACT.Sigmoid)

        share = 1.0 / N_SHIFTS
        bm_share = held.tile([P, 1], F32, name="bm_share")
        nc.vector.tensor_scalar_mul(bm_share[:], bm_sb[:], share)

        def picked(top, n_rows):
            return table_sb[:].indirect(offsets[:, top * ROW_OFFSETS : (top + n_rows) * ROW_OFFSETS])

        msg_ps = []
        for top, n_rows in MSG_PARTS:
            msg_ps.append(psum.tile([P, n_rows * GRID_COLS], F32, name="msg_ps", tag="bank"))
            nc.tensor.matmul(msg_ps[-1][:], wm_sb[:], picked(top, n_rows), start=True, stop=True)

        msg_pad = held.tile([P, PAD_ROWS, PAD_COLS], F32, name="msg_pad")
        first, last = REACH, REACH + GRID_COLS

        def land(part, on_vector=False):
            top, n_rows = MSG_PARTS[part]
            product = as_grid(msg_ps[part][:])
            target = msg_pad[:, top : top + n_rows, :]
            for to_cols, from_cols in (
                (slice(first, last), slice(0, GRID_COLS)),
                (slice(0, first), slice(GRID_COLS - REACH, GRID_COLS)),
                (slice(last, PAD_COLS), slice(0, REACH)),
            ):
                if on_vector:
                    nc.vector.tensor_scalar(
                        target[:, :, to_cols], product[:, :, from_cols], share, bm_share[:], ALU.mult, ALU.add
                    )
                else:
                    nc.scalar.activation(
                        target[:, :, to_cols], product[:, :, from_cols], ACT.Identity, bias=bm_share[:], scale=share
                    )

        for part in range(len(MSG_PARTS)):
            land(part, on_vector=part in VECTOR_LANDS)
        nc.scalar.copy(msg_pad[:, GRID_ROWS:PAD_ROWS, :], msg_pad[:, 0 : PAD_ROWS - GRID_ROWS, :])

        hidden_ps = []
        for top, n_rows in PIECES:
            hidden_ps.append(psum.tile([P, n_rows * GRID_COLS], F32, name="hidden_ps", tag="bank"))
            nc.tensor.matmul(hidden_ps[-1][:], wx_sb[:], picked(top % GRID_ROWS, n_rows), start=True, stop=False)

        DUO_TOP = PIECES[0][0] - STEP[0]
        duo_pad = held.tile([P, STEP[0] + GRID_ROWS, STEP[1] + GRID_COLS], F32, name="duo_pad")

        def make_duo_block(b):
            make_duo(PIECES[0][0] + b * BANK_ROWS, PIECES[0][0] + (b + 1) * BANK_ROWS)

        def make_duo(top, end):
            terms = [
                msg_pad[:, top - dy : end - dy, REACH - STEP[1] - dx : REACH + GRID_COLS - dx]
                for dy, dx in DUO_SHIFTS
            ]
            nc.vector.tensor_tensor(duo_pad[:, top - DUO_TOP : end - DUO_TOP, :], terms[0], terms[1], ALU.add)

        def duo_at(piece, back):
            row = piece[0] - DUO_TOP - STEP[0] * back
            col = STEP[1] * (1 - back)
            return duo_pad[:, row : row + piece[1], col : col + GRID_COLS]

        def pair_on_vector(pair, piece, rows, shifts):
            at = rows[0] - piece[0]
            nc.vector.tensor_tensor(
                as_grid(pair[:])[:, at : at + rows[1], :],
                shifted(msg_pad, rows, shifts[0]),
                shifted(msg_pad, rows, shifts[1]),
                ALU.add,
            )

        def sum_on_tensor(i, shifts):
            helped[i] = psum.tile([P, PIECES[i][1] * GRID_COLS], F32, name="helped_ps", tag="bank")
            for k, shift in enumerate(shifts):
                nc.tensor.matmul(
                    as_grid(helped[i][:]),
                    identity[:],
                    shifted(msg_pad, PIECES[i], shift),
                    start=(k == 0),
                    stop=(k == len(shifts) - 1),
                )

        def first_half_of_gate(i):
            nc.tensor.matmul(hidden_ps[i][:], wa_sb[:], agg_bf[i][:], start=False, stop=True)
            hidden_bf[i] = work.tile([P, PIECES[i][1] * GRID_COLS], BF16, name="hidden_bf")
            nc.scalar.activation(hidden_bf[i][:], hidden_ps[i][:], ACT.Relu, bias=bh_sb[:])

        def second_half_of_gate(i):
            cells = PIECES[i][1] * GRID_COLS
            gate_ps = psum.tile([P, cells], F32, name="gate_ps", tag="bank")
            nc.tensor.matmul(gate_ps[:], wz_sb[:], hidden_bf[i][:], start=True, stop=True)
            gate[i] = work.tile([P, cells], F32, name="gate")
            nc.scalar.activation(gate[i][:], gate_ps[:], ACT.Sigmoid, bias=bz_sb[:])

        far, near, helped, duos, agg, agg_bf, hidden_bf, gate = {}, {}, {}, {}, {}, {}, {}, {}
        far[0] = work.tile([P, PIECES[0][1] * GRID_COLS], F32, name="far")
        near[0] = work.tile([P, PIECES[0][1] * GRID_COLS], F32, name="near")
        for h, half in enumerate(FIRST_HALVES):
            make_duo(half[0] - (STEP[0] if h == 0 else 0), half[0] + half[1])
            pair_on_vector(far[0], PIECES[0], half, FAR_SHIFTS)
            pair_on_vector(near[0], PIECES[0], half, NEAR_SHIFTS)
        for g, group in enumerate(GROUPS):
            if g < len(HELPED):
                sum_on_tensor(HELPED[g], TRIO_SHIFTS if PIECES[HELPED[g]][1] == BANK_ROWS else FAR_SHIFTS)
            if g == 1 or g == 3:
                for i in group:
                    near[i] = work.tile([P, PIECES[i][1] * GRID_COLS], F32, name="near")
                    pair_on_vector(near[i], PIECES[i], PIECES[i], NEAR_SHIFTS)
            if g == 1 or g == 3:
                for i in group:
                    far[i] = work.tile([P, PIECES[i][1] * GRID_COLS], F32, name="far")
                    pair_on_vector(far[i], PIECES[i], PIECES[i], FAR_SHIFTS)
            for i in group:
                duos[i] = work.tile([P, PIECES[i][1] * GRID_COLS], F32, name="duos")
                nc.vector.tensor_tensor(
                    as_grid(duos[i][:]), duo_at(PIECES[i], 0), duo_at(PIECES[i], 1), ALU.add
                )
            for i in group:
                if g == 2:
                    near[i] = helped[i]
                else:
                    nc.vector.tensor_tensor(near[i][:], near[i][:], far[i][:], ALU.add)
            if g + 1 < N_BANKS:
                make_duo_block(g + 1)
            for i in group:
                cells = PIECES[i][1] * GRID_COLS
                agg[i] = work.tile([P, cells], F32, name="agg")
                agg_bf[i] = work.tile([P, cells], BF16, name="agg_bf")
                if PIECES[i][1] == BANK_ROWS:
                    nc.vector.tensor_tensor(agg[i][:], duos[i][:], near[i][:], ALU.add)
                    nc.scalar.copy(agg_bf[i][:], agg[i][:])
                else:
                    nc.vector.tensor_tensor(agg_bf[i][:], duos[i][:], near[i][:], ALU.add)

            if g == len(GROUPS) - 1:
                for i in group:
                    first_half_of_gate(i)
            if g > 0:
                for i in GROUPS[g - 1]:
                    second_half_of_gate(i)
            if g < len(GROUPS) - 1:
                for i in group:
                    first_half_of_gate(i)
        for i in GROUPS[-1]:
            second_half_of_gate(i)

        for i, piece in enumerate(PIECES):
            if piece[1] != BANK_ROWS:
                nc.vector.tensor_tensor(agg[i][:], duos[i][:], near[i][:], ALU.add)
        for i, (top, n_rows) in enumerate(PIECES):
            gated = work.tile([P, n_rows * GRID_COLS], F32, name="gated")
            nc.vector.tensor_tensor(gated[:], agg[i][:], gate[i][:], ALU.mult)
            row = top % GRID_ROWS
            nc.sync.dma_start(out[:, row * GRID_COLS : (row + n_rows) * GRID_COLS], gated[:])
